import numpy as np
import ml_dtypes


def mxq(x, axis, fmt="e4m3"):
    dtype, down = {"e4m3": (ml_dtypes.float8_e4m3fn, 7), "e5m2": (ml_dtypes.float8_e5m2, 14)}[fmt]
    v = np.moveaxis(np.asarray(x, np.float32).astype(ml_dtypes.bfloat16).astype(np.float64), axis, -1)
    blocks = v.reshape(v.shape[:-1] + (-1, 32))
    amax = np.abs(blocks).max(-1, keepdims=True)
    byte = np.maximum(np.where(amax > 0, np.frexp(amax)[1] - 1 + 127, 0) - down, 1)
    scale = np.exp2(byte - 127.0)
    codes = (blocks / scale).astype(np.float32).astype(dtype).astype(np.float64)
    return np.moveaxis((codes * scale).reshape(v.shape), -1, axis)


WIDE = False


def mx_kscale(k):
    if not WIDE:
        return np.ones(k)
    levels = np.array([10, -10, 5, -5, 0])
    if k % 512:
        return np.exp2(np.random.permutation(np.resize(levels, k // 32))).repeat(32)
    a = np.empty((k // 512, 16))
    for p in range(k // 512):
        a[p, :8] = np.random.permutation(np.resize(levels, 8))
        for g in range(8):
            far = levels[np.abs(levels - a[p, g]) >= 10]
            a[p, g + 8] = far[np.random.randint(len(far))]
    return np.exp2(a.ravel()).repeat(32)


BF16 = ml_dtypes.bfloat16


def bf(x):
    return np.asarray(x, np.float32).astype(BF16)


def f64(x):
    return np.asarray(x).astype(np.float64)


B, S, C, HD = 1, 512, 3072, 128
H = C // HD
HP = HD // 2
EPS = 1e-6
THETA = 10000.0


def rmsnorm(h, g):
    return h * (1.0 / np.sqrt(np.mean(h * h, axis=-1, keepdims=True) + EPS)) * g


def apply_rope1(h, freqs):
    sh = h.shape
    h_ = h.reshape(*sh[:-1], -1, 1, 2)
    out = freqs[..., 0] * h_[..., 0] + freqs[..., 1] * h_[..., 1]
    return out.reshape(sh)


def draw0():
    s = mx_kscale(C)
    pos = f64(np.random.randint(0, S, size=(S, 1)))
    inv_freq = 1.0 / THETA ** (np.arange(HP) / HP)
    ang = pos * inv_freq
    cos, sin = np.cos(ang), np.sin(ang)
    rot = np.stack([np.stack([cos, -sin], -1), np.stack([sin, cos], -1)], -2)
    return {"x": bf(np.random.standard_normal((B, S, C)) * s),
            "freqs": bf(rot[None, :, None]),
            "w": bf(np.random.standard_normal((C, C)) / np.sqrt(C) / s[None, :]),
            "b": bf(np.random.standard_normal(C) * 0.3),
            "g": bf(1.0 + 0.1 * np.random.standard_normal(HD))}


def core(x, freqs, w, b, g):
    p = (mxq(f64(x), 2, "e4m3") @ mxq(f64(w), 1, "e4m3").T) + f64(b)
    h = p.reshape(B, S, H, HD)
    return apply_rope1(rmsnorm(h, f64(g)), f64(freqs))


def e4m3fn_bytes(y):
    return np.clip(np.asarray(y, np.float64), -448.0, 448.0).astype(np.float32).astype(ml_dtypes.float8_e4m3fn).view(np.uint8)


def e4m3fn_values(b):
    return np.asarray(b, np.uint8).view(ml_dtypes.float8_e4m3fn).astype(np.float64)


def setup_inputs():
    d = draw0()
    x0 = np.asarray(d['w']).astype(np.float64)
    s = (np.max(np.abs(x0), axis=(0,), keepdims=True) / 448.0).astype(np.float32)
    out = {}
    for k, v in d.items():
        if k == 'w':
            out['w_bytes'] = e4m3fn_bytes(x0 / s.astype(np.float64))
            out['w_scale'] = s
        else:
            out[k] = v
    return out


def reference(x, freqs, w_bytes, w_scale, b, g):
    return core(x, freqs, e4m3fn_values(w_bytes) * w_scale.astype(np.float64), b, g)

@@ -1,0 +1,278 @@
+from contextlib import ExitStack
+
+import concourse.mybir as mybir
+from concourse.masks import make_identity
+
+F32 = mybir.dt.float32
+BF16 = mybir.dt.bfloat16
+U32 = mybir.dt.uint32
+U8 = mybir.dt.uint8
+FP8 = mybir.dt.float8_e4m3fn
+FP8X4 = mybir.dt.float8_e4m3fn_x4
+ACT = mybir.ActivationFunctionType
+ALU = mybir.AluOpType
+
+P = 128
+K = 3072
+TOKENS = 512
+CHANNELS = 3072
+HEAD = 128
+EPS = 1e-6
+PASSES = K // 512
+PAIRS = PASSES // 2
+M_TILES = TOKENS // P
+ROW_TILES = CHANNELS // P
+GROUP_TILES = (4, 4, 4, 4, 4, 2, 2)
+RUN = 3
+PREFETCH = 6
+
+FLOPS = 2 * TOKENS * K * CHANNELS
+
+
+def quantize_widths(total):
+    widths = []
+    while total > 0:
+        w = 4096
+        while w > total:
+            w //= 2
+        widths.append(w)
+        total -= w
+    return widths
+
+
+def tile_selfattention_pa_kernel(tc, x, freqs, w_bytes, w_scale, b, g, out):
+    nc = tc.nc
+    x_rows = x.rearrange("o s k -> (o s) k")
+    out_rows = out.rearrange("o s h d -> (o s) (h d)")
+    fr_rows = freqs.rearrange("o s a j i l -> (o s a) (j i l)")
+
+    with ExitStack() as ctx:
+        const = ctx.enter_context(tc.tile_pool(name="const", bufs=1))
+        wbytes = ctx.enter_context(tc.tile_pool(name="wbytes", bufs=PREFETCH + 2))
+        rows = ctx.enter_context(tc.tile_pool(name="rows", bufs=8))
+        grouped = ctx.enter_context(tc.tile_pool(name="grouped", bufs=2))
+        wq = ctx.enter_context(tc.tile_pool(name="wq", bufs=2))
+        proj = ctx.enter_context(tc.tile_pool(name="proj", bufs=6))
+        epi = ctx.enter_context(tc.tile_pool(name="epi", bufs=5))
+        small = ctx.enter_context(tc.tile_pool(name="small", bufs=6))
+        banks = ctx.enter_context(tc.psum_pool(name="banks", bufs=6))
+        accs = ctx.enter_context(tc.psum_pool(name="accs", bufs=2))
+
+        k_scale = const.tile([P, PASSES, 4], F32, name="k_scale")
+        nc.scalar.dma_start(out=k_scale[:], in_=w_scale.rearrange("o (g p t) -> p (o g) t", p=P, t=4))
+        fr_sb = const.tile([P, M_TILES, 256], BF16, name="fr_sb")
+        nc.scalar.dma_start(out=fr_sb[:], in_=fr_rows.rearrange("(m p) c -> p m c", p=P))
+        g_bc = const.tile([P, HEAD], BF16, name="g_bc")
+        nc.scalar.dma_start(out=g_bc[:], in_=g.partition_broadcast(P))
+
+        one = const.tile([P, 1], F32, name="one")
+        nc.gpsimd.memset(one[:], 1.0)
+        warm = const.tile([P, 1], F32, name="warm")
+        nc.scalar.activation(out=warm[:], in_=one[:], func=ACT.Abs_reciprocal_sqrt)
+
+        ident = const.tile([P, P], F32, name="ident")
+        make_identity(nc, ident[:])
+
+        def load_w(i):
+            wb = wbytes.tile([P, K], U8, name="wb", tag="wb")
+            nc.sync.dma_start(out=wb[:], in_=w_bytes[i * P : (i + 1) * P, :])
+            return wb
+
+        def load_x(m):
+            xr = rows.tile([P, K], BF16, name="xr", tag="rows")
+            nc.sync.dma_start(out=xr[:], in_=x_rows[m * P : (m + 1) * P, :])
+            return xr
+
+        wb_tiles = {}
+        x_tiles = {}
+        for i in (0, 1):
+            wb_tiles[i] = wbytes.tile([P, K], U8, name="wb", tag="wb")
+        for c0, c1 in ((0, 1024), (1024, K)):
+            for i in (0, 1):
+                nc.sync.dma_start(out=wb_tiles[i][:, c0:c1], in_=w_bytes[i * P : (i + 1) * P, c0:c1])
+        for m in range(M_TILES):
+            x_tiles[m] = load_x(m)
+        for i in range(2, PREFETCH):
+            wb_tiles[i] = load_w(i)
+        b_bc = const.tile([P, CHANNELS], BF16, name="b_bc")
+        nc.sync.dma_start(out=b_bc[:], in_=b.partition_broadcast(P))
+
+        rot = []
+        fr_v = fr_sb[:].rearrange("p m (j i l) -> p m j i l", i=2, l=2)
+        g_v = g_bc[:].rearrange("p (j l) -> p j l", l=2)
+        for l in (0, 1):
+            rl = const.tile([P, M_TILES, HEAD], F32, name="rot%d" % l)
+            nc.gpsimd.tensor_tensor(
+                out=rl[:].rearrange("p m (j i) -> p m j i", i=2),
+                in0=fr_v[:, :, :, :, l],
+                in1=g_v[:, :, l].unsqueeze(1).unsqueeze(3).to_broadcast([P, M_TILES, HEAD // 2, 2]),
+                op=ALU.mult,
+            )
+            rot.append(rl)
+
+        x_codes = const.tile([P, M_TILES * PASSES * P], U32, name="x_codes", align_bytes=64)
+        x_scales = const.tile([P, M_TILES * PASSES * P], U8, name="x_scales", align_bytes=64)
+
+        def transpose_pass(two_tiles, gp):
+            bank = banks.tile([P, 512], F32, name="bank", tag="bank")
+            for u in (0, 1):
+                for rr in (0, 1):
+                    col = (2 * u + rr) * P
+                    nc.tensor.transpose(
+                        out=bank[:, col : col + P],
+                        in_=two_tiles[rr][:].bitcast(F32)[:, 256 * gp + u : 256 * (gp + 1) : 2],
+                        identity=ident[:],
+                    )
+            return bank
+
+        def quantize(src, codes, scales, first_word):
+            col = 0
+            for w in quantize_widths(src.shape[1]):
+                words = slice(first_word + col // 4, first_word + (col + w) // 4)
+                nc.vector.quantize_mx(out=codes[:, words].bitcast(FP8X4), scales=scales[:, words], in_=src[:, col : col + w])
+                col += w
+
+        def x_stage(mp):
+            two = (x_tiles[2 * mp], x_tiles[2 * mp + 1])
+            gx = grouped.tile([P, 2 * K], BF16, name="gx", tag="gx", bufs=1, align_bytes=64)
+            for gp in range(PASSES):
+                bank = transpose_pass(two, gp)
+                mover = nc.vector.tensor_copy if mp == 0 else nc.scalar.copy
+                mover(
+                    out=gx[:, gp * 1024 : (gp + 1) * 1024].bitcast(F32).rearrange("p (n u) -> p n u", u=2),
+                    in_=bank[:].rearrange("p (u n) -> p n u", u=2),
+                )
+            quantize(gx, x_codes, x_scales, mp * 2 * PASSES * P)
+
+        def new_pair():
+            return [rows.tile([P, K], BF16, name="wr", tag="rows") for rr in (0, 1)]
+
+        def cast_cols(i, two, c0, c1):
+            for rr in (0, 1):
+                nc.scalar.copy(out=two[rr][:, c0:c1], in_=wb_tiles[i + rr][:, c0:c1].bitcast(FP8))
+
+        def scale_out(bank, grp, n_tiles, r, gp):
+            col = (gp * n_tiles + r) * 512
+            nc.vector.tensor_tensor(
+                out=grp[:, col : col + 1024].rearrange("p (n u e) -> p n u e", u=2, e=2),
+                in0=bank[:].bitcast(BF16).rearrange("p (u n e) -> p n u e", u=2, e=2),
+                in1=k_scale[:, gp, :].rearrange("p (u e) -> p u e", e=2).unsqueeze(1).to_broadcast([P, 2 * P, 2, 2]),
+                op=ALU.mult,
+            )
+
+        def epilogue(first, n_tiles, m, acc, on_vector):
+            eng = nc.vector if on_vector else nc.gpsimd
+            width = n_tiles * P
+            shape4 = [P, n_tiles, HEAD // 2, 2]
+            c0 = first * P
+            pr = proj.tile([P, width], F32, name="pr", tag="pr")
+            nc.vector.tensor_tensor(out=pr[:], in0=acc[:], in1=b_bc[:, c0 : c0 + width], op=ALU.add)
+            ss = small.tile([P, n_tiles], F32, name="ss", tag="ss")
+            for h in range(n_tiles):
+                junk = small.tile([P, HEAD], F32, name="junk", tag="junk")
+                nc.scalar.activation(
+                    out=junk[:], in_=pr[:, h * HEAD : (h + 1) * HEAD], func=ACT.Square, accum_out=ss[:, h : h + 1]
+                )
+            rinv = small.tile([P, n_tiles], F32, name="rinv", tag="rinv")
+            nc.scalar.activation(out=rinv[:], in_=ss[:], func=ACT.Abs_reciprocal_sqrt, bias=EPS, scale=1.0 / HEAD)
+
+            pv = pr[:].rearrange("p (h j l) -> p h j l", h=n_tiles, l=2)
+            terms = []
+            for l in (0, 1):
+                t = epi.tile([P, width], F32, name="term%d" % l, tag="term%d" % l)
+                eng.tensor_tensor(
+                    out=t[:].rearrange("p (h j i) -> p h j i", h=n_tiles, i=2),
+                    in0=pv[:, :, :, l : l + 1].to_broadcast(shape4),
+                    in1=rot[l][:, m, :].rearrange("p (j i) -> p j i", i=2).unsqueeze(1).to_broadcast(shape4),
+                    op=ALU.mult,
+                )
+                terms.append(t)
+            res = terms[0]
+            eng.tensor_tensor(out=res[:], in0=terms[0][:], in1=terms[1][:], op=ALU.add)
+            waiting.append((res, rinv, n_tiles, m, c0))
+            if len(waiting) - finished[0] > 1:
+                finish()
+
+        waiting = []
+        finished = [0]
+
+        def finish():
+            res, rinv, n_tiles, m, c0 = waiting[finished[0]]
+            finished[0] += 1
+            for h in range(n_tiles):
+                cols = slice(h * HEAD, (h + 1) * HEAD)
+                nc.scalar.activation(out=res[:, cols], in_=res[:, cols], func=ACT.Copy, scale=rinv[:, h : h + 1])
+            nc.sync.dma_start(out=out_rows[m * P : (m + 1) * P, c0 : c0 + n_tiles * P], in_=res[:])
+
+        open_acc = {}
+
+        def run_pass(item):
+            first, n_tiles, codes, scales, m, gp, on_vector = item
+            width = n_tiles * P
+            if gp == 0:
+                open_acc[m] = accs.tile([P, width], F32, name="acc", tag="acc")
+            acc = open_acc[m]
+            xw = ((m // 2) * 2 * PASSES + gp * 2 + m % 2) * P
+            xc = slice(xw, xw + P)
+            wc = slice(gp * width, (gp + 1) * width)
+            nc.tensor.matmul_mx(
+                out=acc[:],
+                lhsT=x_codes[:, xc].bitcast(FP8X4),
+                lhsT_scale=x_scales[:, xc],
+                rhs=codes[:, wc].bitcast(FP8X4),
+                rhs_scale=scales[:, wc],
+                start=(gp == 0),
+                stop=(gp == PASSES - 1),
+            )
+            if gp == PASSES - 1:
+                epilogue(first, n_tiles, m, acc, on_vector)
+
+        todo = []
+        st = {"done": 0, "first": 0}
+
+        def run_group(gi):
+            n_tiles = GROUP_TILES[gi]
+            first = st["first"]
+            grp = grouped.tile([P, PASSES * n_tiles * 512], BF16, name="grp", tag="grp", align_bytes=64)
+            slots = PAIRS * n_tiles // RUN
+            for r in range(0, n_tiles, 2):
+                i = first + r
+                for j in (i + PREFETCH, i + PREFETCH + 1):
+                    if j < ROW_TILES:
+                        wb_tiles[j] = load_w(j)
+                two = st["two_next"]
+                if i + 2 < ROW_TILES:
+                    st["two_next"] = new_pair()
+                for gp in range(PASSES):
+                    if gp % 2 == 0 and i + 2 < ROW_TILES:
+                        cast_cols(i + 2, st["two_next"], gp * 512, gp * 512 + 1024)
+                    bank = transpose_pass(two, gp)
+                    scale_out(bank, grp, n_tiles, r, gp)
+                    if gp % RUN == RUN - 1:
+                        share = -((st["done"] - len(todo)) // slots)
+                        for item in todo[st["done"] : st["done"] + share]:
+                            run_pass(item)
+                        st["done"] += share
+                        slots -= 1
+                if i < M_TILES:
+                    x_stage(i // 2)
+            codes = wq.tile([P, PASSES * n_tiles * P], U32, name="w_codes", tag="w_codes", align_bytes=64)
+            scales = wq.tile([P, PASSES * n_tiles * P], U8, name="w_scales", tag="w_scales", align_bytes=64)
+            quantize(grp, codes, scales, 0)
+            last = gi == len(GROUP_TILES) - 1
+            for m in range(M_TILES):
+                for gp in range(PASSES):
+                    todo.append((first, n_tiles, codes, scales, m, gp, last and m != 1))
+            st["first"] = first + n_tiles
+
+        with tc.manual_schedule(engines={mybir.EngineType.PE}):
+            st["two_next"] = new_pair()
+            for c0 in range(0, K, 512):
+                cast_cols(0, st["two_next"], c0, c0 + 512)
+            run_group(0)
+        with tc.manual_schedule(engines={mybir.EngineType.PE, mybir.EngineType.Activation}):
+            for gi in range(1, len(GROUP_TILES)):
+                run_group(gi)
+            for item in todo[st["done"] :]:
+                run_pass(item)
+            finish()

@@ -160,6 +160,15 @@ def tile_selfattention_pa_kernel(tc, x, freqs, w_bytes, w_scale, b, g, out):
                 op=ALU.mult,
             )
 
+        def scale_out_scalar(bank, grp, n_tiles, r, gp):
+            col = (gp * n_tiles + r) * 512
+            dst = grp[:, col : col + 1024].rearrange("p (n t) -> p n t", t=4)
+            srcv = bank[:].bitcast(BF16).rearrange("p (u n e) -> p n u e", u=2, e=2)
+            for u in (0, 1):
+                for e in (0, 1):
+                    t = 2 * u + e
+                    nc.scalar.activation(out=dst[:, :, t], in_=srcv[:, :, u, e], func=ACT.Copy, scale=k_scale[:, gp, t : t + 1])
+
         def epilogue(first, n_tiles, m, acc, on_vector):
             eng = nc.vector if on_vector else nc.gpsimd
             width = n_tiles * P
@@ -247,7 +256,10 @@ def tile_selfattention_pa_kernel(tc, x, freqs, w_bytes, w_scale, b, g, out):
                     if gp % 2 == 0 and i + 2 < ROW_TILES:
                         cast_cols(i + 2, st["two_next"], gp * 512, gp * 512 + 1024)
                     bank = transpose_pass(two, gp)
-                    scale_out(bank, grp, n_tiles, r, gp)
+                    if gi > 0 and r == n_tiles - 2 and gp == 0:
+                        scale_out_scalar(bank, grp, n_tiles, r, gp)
+                    else:
+                        scale_out(bank, grp, n_tiles, r, gp)
                     if gp % RUN == RUN - 1:
                         share = -((st["done"] - len(todo)) // slots)
                         for item in todo[st["done"] : st["done"] + share]:

@@ -256,7 +256,7 @@ def tile_selfattention_pa_kernel(tc, x, freqs, w_bytes, w_scale, b, g, out):
                     if gp % 2 == 0 and i + 2 < ROW_TILES:
                         cast_cols(i + 2, st["two_next"], gp * 512, gp * 512 + 1024)
                     bank = transpose_pass(two, gp)
-                    if gi > 0 and r == n_tiles - 2 and gp == 0:
+                    if (gi % 2 == 1 or gi == len(GROUP_TILES) - 1) and r == n_tiles - 2 and gp == 0:
                         scale_out_scalar(bank, grp, n_tiles, r, gp)
                     else:
                         scale_out(bank, grp, n_tiles, r, gp)

@@ -25,6 +25,7 @@ ROW_TILES = CHANNELS // P
 GROUP_TILES = (4, 4, 4, 4, 4, 2, 2)
 RUN = 3
 PREFETCH = 6
+HELPED = (3,)
 
 FLOPS = 2 * TOKENS * K * CHANNELS
 
@@ -55,7 +56,8 @@ def tile_selfattention_pa_kernel(tc, x, freqs, w_bytes, w_scale, b, g, out):
         proj = ctx.enter_context(tc.tile_pool(name="proj", bufs=6))
         epi = ctx.enter_context(tc.tile_pool(name="epi", bufs=5))
         small = ctx.enter_context(tc.tile_pool(name="small", bufs=6))
-        banks = ctx.enter_context(tc.psum_pool(name="banks", bufs=6))
+        banks = ctx.enter_context(tc.psum_pool(name="banks", bufs=5))
+        tabs = ctx.enter_context(tc.psum_pool(name="tabs", bufs=1))
         accs = ctx.enter_context(tc.psum_pool(name="accs", bufs=2))
 
         k_scale = const.tile([P, PASSES, 4], F32, name="k_scale")
@@ -109,6 +111,22 @@ def tile_selfattention_pa_kernel(tc, x, freqs, w_bytes, w_scale, b, g, out):
                 op=ALU.mult,
             )
             rot.append(rl)
+
+        rot_turned = const.tile([P, 2 * len(HELPED) * HEAD], F32, name="rot_turned")
+        rot_ps = tabs.tile([P, 2 * len(HELPED) * HEAD], F32, name="rot_ps")
+
+        def tables_first_turn():
+            bank = banks.tile([P, 512], F32, name="bank", tag="bank")
+            for l in (0, 1):
+                for q, m in enumerate(HELPED):
+                    col = (l * len(HELPED) + q) * HEAD
+                    nc.tensor.transpose(out=bank[:, col : col + HEAD], in_=rot[l][:, m, :], identity=ident[:])
+            nc.vector.tensor_copy(out=rot_turned[:], in_=bank[:, : 2 * len(HELPED) * HEAD])
+
+        def tables_second_turn():
+            for c in range(2 * len(HELPED)):
+                cols = slice(c * HEAD, (c + 1) * HEAD)
+                nc.tensor.transpose(out=rot_ps[:, cols], in_=rot_turned[:, cols], identity=ident[:])
 
         x_codes = const.tile([P, M_TILES * PASSES * P], U32, name="x_codes", align_bytes=64)
         x_scales = const.tile([P, M_TILES * PASSES * P], U8, name="x_scales", align_bytes=64)
@@ -189,10 +207,15 @@ def tile_selfattention_pa_kernel(tc, x, freqs, w_bytes, w_scale, b, g, out):
             terms = []
             for l in (0, 1):
                 t = epi.tile([P, width], F32, name="term%d" % l, tag="term%d" % l)
-                eng.tensor_tensor(
+                if m in HELPED:
+                    col = (l * len(HELPED) + HELPED.index(m)) * HEAD
+                    multiplier, table = nc.vector, rot_ps[:, col : col + HEAD]
+                else:
+                    multiplier, table = eng, rot[l][:, m, :]
+                multiplier.tensor_tensor(
                     out=t[:].rearrange("p (h j i) -> p h j i", h=n_tiles, i=2),
                     in0=pv[:, :, :, l : l + 1].to_broadcast(shape4),
-                    in1=rot[l][:, m, :].rearrange("p (j i) -> p j i", i=2).unsqueeze(1).to_broadcast(shape4),
+                    in1=table.rearrange("p (j i) -> p j i", i=2).unsqueeze(1).to_broadcast(shape4),
                     op=ALU.mult,
                 )
                 terms.append(t)
@@ -268,6 +291,10 @@ def tile_selfattention_pa_kernel(tc, x, freqs, w_bytes, w_scale, b, g, out):
                         slots -= 1
                 if i < M_TILES:
                     x_stage(i // 2)
+                    if i == 0:
+                        tables_first_turn()
+                    else:
+                        tables_second_turn()
             codes = wq.tile([P, PASSES * n_tiles * P], U32, name="w_codes", tag="w_codes", align_bytes=64)
             scales = wq.tile([P, PASSES * n_tiles * P], U8, name="w_scales", tag="w_scales", align_bytes=64)
             quantize(grp, codes, scales, 0)

@@ -266,7 +266,8 @@ def tile_selfattention_pa_kernel(tc, x, freqs, w_bytes, w_scale, b, g, out):
             n_tiles = GROUP_TILES[gi]
             first = st["first"]
             grp = grouped.tile([P, PASSES * n_tiles * 512], BF16, name="grp", tag="grp", align_bytes=64)
-            slots = PAIRS * n_tiles // RUN
+            stops = (1, 4, 7, 10) if n_tiles == 4 else (1, 4)
+            slots = len(stops)
             for r in range(0, n_tiles, 2):
                 i = first + r
                 for j in (i + PREFETCH, i + PREFETCH + 1):
@@ -283,7 +284,7 @@ def tile_selfattention_pa_kernel(tc, x, freqs, w_bytes, w_scale, b, g, out):
                         scale_out_scalar(bank, grp, n_tiles, r, gp)
                     else:
                         scale_out(bank, grp, n_tiles, r, gp)
-                    if gp % RUN == RUN - 1:
+                    if (r // 2) * PASSES + gp in stops:
                         share = -((st["done"] - len(todo)) // slots)
                         for item in todo[st["done"] : st["done"] + share]:
                             run_pass(item)

@@ -219,11 +219,28 @@ def tile_selfattention_pa_kernel(tc, x, freqs, w_bytes, w_scale, b, g, out):
                     op=ALU.mult,
                 )
                 terms.append(t)
+            unit = (eng, terms, rinv, n_tiles, m, c0)
+            if m in HELPED and first + n_tiles < ROW_TILES:
+                held.append(unit)
+            else:
+                add_terms(unit)
+
+        def add_terms(unit):
+            eng, terms, rinv, n_tiles, m, c0 = unit
             res = terms[0]
             eng.tensor_tensor(out=res[:], in0=terms[0][:], in1=terms[1][:], op=ALU.add)
             waiting.append((res, rinv, n_tiles, m, c0))
             if len(waiting) - finished[0] > 1:
                 finish()
+
+        held = []
+
+        def release_held(codes):
+            if held:
+                seen = small.tile([P, 1], U32, name="seen", tag="seen")
+                nc.gpsimd.tensor_copy(out=seen[:], in_=codes[:, codes.shape[1] - 1 :])
+                add_terms(held[0])
+                held.clear()
 
         waiting = []
         finished = [0]
@@ -299,6 +316,7 @@ def tile_selfattention_pa_kernel(tc, x, freqs, w_bytes, w_scale, b, g, out):
             codes = wq.tile([P, PASSES * n_tiles * P], U32, name="w_codes", tag="w_codes", align_bytes=64)
             scales = wq.tile([P, PASSES * n_tiles * P], U8, name="w_scales", tag="w_scales", align_bytes=64)
             quantize(grp, codes, scales, 0)
+            release_held(codes)
             last = gi == len(GROUP_TILES) - 1
             for m in range(M_TILES):
                 for gp in range(PASSES):
@@ -310,7 +328,7 @@ def tile_selfattention_pa_kernel(tc, x, freqs, w_bytes, w_scale, b, g, out):
             for c0 in range(0, K, 512):
                 cast_cols(0, st["two_next"], c0, c0 + 512)
             run_group(0)
-        with tc.manual_schedule(engines={mybir.EngineType.PE, mybir.EngineType.Activation}):
+        with tc.manual_schedule(engines={mybir.EngineType.PE, mybir.EngineType.Activation, mybir.EngineType.Pool}):
             for gi in range(1, len(GROUP_TILES)):
                 run_group(gi)
             for item in todo[st["done"] :]:

@@ -19,13 +19,11 @@ CHANNELS = 3072
 HEAD = 128
 EPS = 1e-6
 PASSES = K // 512
-PAIRS = PASSES // 2
 M_TILES = TOKENS // P
 ROW_TILES = CHANNELS // P
 GROUP_TILES = (4, 4, 4, 4, 4, 2, 2)
-RUN = 3
+LAST = len(GROUP_TILES) - 1
 PREFETCH = 6
-HELPED = (3,)
 
 FLOPS = 2 * TOKENS * K * CHANNELS
 
@@ -53,9 +51,9 @@ def tile_selfattention_pa_kernel(tc, x, freqs, w_bytes, w_scale, b, g, out):
         rows = ctx.enter_context(tc.tile_pool(name="rows", bufs=8))
         grouped = ctx.enter_context(tc.tile_pool(name="grouped", bufs=2))
         wq = ctx.enter_context(tc.tile_pool(name="wq", bufs=2))
-        proj = ctx.enter_context(tc.tile_pool(name="proj", bufs=6))
-        epi = ctx.enter_context(tc.tile_pool(name="epi", bufs=5))
-        small = ctx.enter_context(tc.tile_pool(name="small", bufs=6))
+        proj = ctx.enter_context(tc.tile_pool(name="proj", bufs=7))
+        epi = ctx.enter_context(tc.tile_pool(name="epi", bufs=6))
+        small = ctx.enter_context(tc.tile_pool(name="small", bufs=8))
         banks = ctx.enter_context(tc.psum_pool(name="banks", bufs=5))
         tabs = ctx.enter_context(tc.psum_pool(name="tabs", bufs=1))
         accs = ctx.enter_context(tc.psum_pool(name="accs", bufs=2))
@@ -92,10 +90,14 @@ def tile_selfattention_pa_kernel(tc, x, freqs, w_bytes, w_scale, b, g, out):
         for c0, c1 in ((0, 1024), (1024, K)):
             for i in (0, 1):
                 nc.sync.dma_start(out=wb_tiles[i][:, c0:c1], in_=w_bytes[i * P : (i + 1) * P, c0:c1])
-        for m in range(M_TILES):
-            x_tiles[m] = load_x(m)
-        for i in range(2, PREFETCH):
-            wb_tiles[i] = load_w(i)
+        x_tiles[0] = load_x(0)
+        x_tiles[1] = load_x(1)
+        wb_tiles[2] = load_w(2)
+        wb_tiles[3] = load_w(3)
+        x_tiles[2] = load_x(2)
+        x_tiles[3] = load_x(3)
+        wb_tiles[4] = load_w(4)
+        wb_tiles[5] = load_w(5)
         b_bc = const.tile([P, CHANNELS], BF16, name="b_bc")
         nc.sync.dma_start(out=b_bc[:], in_=b.partition_broadcast(P))
 
@@ -112,19 +114,19 @@ def tile_selfattention_pa_kernel(tc, x, freqs, w_bytes, w_scale, b, g, out):
             )
             rot.append(rl)
 
-        rot_turned = const.tile([P, 2 * len(HELPED) * HEAD], F32, name="rot_turned")
-        rot_ps = tabs.tile([P, 2 * len(HELPED) * HEAD], F32, name="rot_ps")
+        rot_turned = const.tile([P, 4 * HEAD], F32, name="rot_turned")
+        rot_ps = tabs.tile([P, 4 * HEAD], F32, name="rot_ps")
 
         def tables_first_turn():
             bank = banks.tile([P, 512], F32, name="bank", tag="bank")
-            for l in (0, 1):
-                for q, m in enumerate(HELPED):
-                    col = (l * len(HELPED) + q) * HEAD
+            for m in (2, 3):
+                for l in (0, 1):
+                    col = (2 * (m - 2) + l) * HEAD
                     nc.tensor.transpose(out=bank[:, col : col + HEAD], in_=rot[l][:, m, :], identity=ident[:])
-            nc.vector.tensor_copy(out=rot_turned[:], in_=bank[:, : 2 * len(HELPED) * HEAD])
+            nc.vector.tensor_copy(out=rot_turned[:], in_=bank[:])
 
         def tables_second_turn():
-            for c in range(2 * len(HELPED)):
+            for c in range(4):
                 cols = slice(c * HEAD, (c + 1) * HEAD)
                 nc.tensor.transpose(out=rot_ps[:, cols], in_=rot_turned[:, cols], identity=ident[:])
 
@@ -143,10 +145,10 @@ def tile_selfattention_pa_kernel(tc, x, freqs, w_bytes, w_scale, b, g, out):
                     )
             return bank
 
-        def quantize(src, codes, scales, first_word):
-            col = 0
-            for w in quantize_widths(src.shape[1]):
-                words = slice(first_word + col // 4, first_word + (col + w) // 4)
+        def quantize(src, first_col, n_cols, codes, scales, first_word):
+            col = first_col
+            for w in quantize_widths(n_cols):
+                words = slice(first_word + (col - first_col) // 4, first_word + (col - first_col + w) // 4)
                 nc.vector.quantize_mx(out=codes[:, words].bitcast(FP8X4), scales=scales[:, words], in_=src[:, col : col + w])
                 col += w
 
@@ -160,7 +162,7 @@ def tile_selfattention_pa_kernel(tc, x, freqs, w_bytes, w_scale, b, g, out):
                     out=gx[:, gp * 1024 : (gp + 1) * 1024].bitcast(F32).rearrange("p (n u) -> p n u", u=2),
                     in_=bank[:].rearrange("p (u n) -> p n u", u=2),
                 )
-            quantize(gx, x_codes, x_scales, mp * 2 * PASSES * P)
+            quantize(gx, 0, 2 * K, x_codes, x_scales, mp * 2 * PASSES * P)
 
         def new_pair():
             return [rows.tile([P, K], BF16, name="wr", tag="rows") for rr in (0, 1)]
@@ -178,22 +180,16 @@ def tile_selfattention_pa_kernel(tc, x, freqs, w_bytes, w_scale, b, g, out):
                 op=ALU.mult,
             )
 
-        def scale_out_scalar(bank, grp, n_tiles, r, gp):
-            col = (gp * n_tiles + r) * 512
-            dst = grp[:, col : col + 1024].rearrange("p (n t) -> p n t", t=4)
-            srcv = bank[:].bitcast(BF16).rearrange("p (u n e) -> p n u e", u=2, e=2)
-            for u in (0, 1):
-                for e in (0, 1):
-                    t = 2 * u + e
-                    nc.scalar.activation(out=dst[:, :, t], in_=srcv[:, :, u, e], func=ACT.Copy, scale=k_scale[:, gp, t : t + 1])
+        waiting = []
+        finished = [0]
+        held = []
 
-        def epilogue(first, n_tiles, m, acc, on_vector):
-            eng = nc.vector if on_vector else nc.gpsimd
+        def project(gi, first, n_tiles, m, acc):
             width = n_tiles * P
-            shape4 = [P, n_tiles, HEAD // 2, 2]
             c0 = first * P
+            last = gi == LAST
             pr = proj.tile([P, width], F32, name="pr", tag="pr")
-            nc.vector.tensor_tensor(out=pr[:], in0=acc[:], in1=b_bc[:, c0 : c0 + width], op=ALU.add)
+            nc.vector.tensor_tensor(out=pr[:], in0=acc, in1=b_bc[:, c0 : c0 + width], op=ALU.add)
             ss = small.tile([P, n_tiles], F32, name="ss", tag="ss")
             for h in range(n_tiles):
                 junk = small.tile([P, HEAD], F32, name="junk", tag="junk")
@@ -202,17 +198,21 @@ def tile_selfattention_pa_kernel(tc, x, freqs, w_bytes, w_scale, b, g, out):
                 )
             rinv = small.tile([P, n_tiles], F32, name="rinv", tag="rinv")
             nc.scalar.activation(out=rinv[:], in_=ss[:], func=ACT.Abs_reciprocal_sqrt, bias=EPS, scale=1.0 / HEAD)
+            unit = (gi, pr, rinv, n_tiles, m, c0)
+            rotate(unit)
 
+        def rotate(unit):
+            gi, pr, rinv, n_tiles, m, c0 = unit
+            last = gi == LAST
+            helped = m == 3 or (m == 2 and gi >= 4)
+            eng = nc.vector if last and m != 1 else nc.gpsimd
+            shape4 = [P, n_tiles, HEAD // 2, 2]
             pv = pr[:].rearrange("p (h j l) -> p h j l", h=n_tiles, l=2)
             terms = []
             for l in (0, 1):
-                t = epi.tile([P, width], F32, name="term%d" % l, tag="term%d" % l)
-                if m in HELPED:
-                    col = (l * len(HELPED) + HELPED.index(m)) * HEAD
-                    multiplier, table = nc.vector, rot_ps[:, col : col + HEAD]
-                else:
-                    multiplier, table = eng, rot[l][:, m, :]
-                multiplier.tensor_tensor(
+                t = epi.tile([P, n_tiles * P], F32, name="term%d" % l, tag="term%d" % l)
+                table = rot_ps[:, (2 * (m - 2) + l) * HEAD : (2 * (m - 2) + l + 1) * HEAD] if helped else rot[l][:, m, :]
+                (nc.vector if helped else eng).tensor_tensor(
                     out=t[:].rearrange("p (h j i) -> p h j i", h=n_tiles, i=2),
                     in0=pv[:, :, :, l : l + 1].to_broadcast(shape4),
                     in1=table.rearrange("p (j i) -> p j i", i=2).unsqueeze(1).to_broadcast(shape4),
@@ -220,20 +220,28 @@ def tile_selfattention_pa_kernel(tc, x, freqs, w_bytes, w_scale, b, g, out):
                 )
                 terms.append(t)
             unit = (eng, terms, rinv, n_tiles, m, c0)
-            if m in HELPED and first + n_tiles < ROW_TILES:
+            if m == 3 and not last:
                 held.append(unit)
             else:
                 add_terms(unit)
 
         def add_terms(unit):
             eng, terms, rinv, n_tiles, m, c0 = unit
-            res = terms[0]
-            eng.tensor_tensor(out=res[:], in0=terms[0][:], in1=terms[1][:], op=ALU.add)
-            waiting.append((res, rinv, n_tiles, m, c0))
+            eng.tensor_tensor(out=terms[0][:], in0=terms[0][:], in1=terms[1][:], op=ALU.add)
+            close(terms[0], terms[0], rinv, n_tiles, m, c0)
+
+        def close(src, res, rinv, n_tiles, m, c0):
+            waiting.append((src, res, rinv, n_tiles, m, c0))
             if len(waiting) - finished[0] > 1:
                 finish()
 
-        held = []
+        def finish():
+            src, res, rinv, n_tiles, m, c0 = waiting[finished[0]]
+            finished[0] += 1
+            for h in range(n_tiles):
+                cols = slice(h * HEAD, (h + 1) * HEAD)
+                nc.scalar.activation(out=res[:, cols], in_=src[:, cols], func=ACT.Copy, scale=rinv[:, h : h + 1])
+            nc.sync.dma_start(out=out_rows[m * P : (m + 1) * P, c0 : c0 + n_tiles * P], in_=res[:])
 
         def release_held(codes):
             if held:
@@ -242,30 +250,24 @@ def tile_selfattention_pa_kernel(tc, x, freqs, w_bytes, w_scale, b, g, out):
                 add_terms(held[0])
                 held.clear()
 
-        waiting = []
-        finished = [0]
-
-        def finish():
-            res, rinv, n_tiles, m, c0 = waiting[finished[0]]
-            finished[0] += 1
-            for h in range(n_tiles):
-                cols = slice(h * HEAD, (h + 1) * HEAD)
-                nc.scalar.activation(out=res[:, cols], in_=res[:, cols], func=ACT.Copy, scale=rinv[:, h : h + 1])
-            nc.sync.dma_start(out=out_rows[m * P : (m + 1) * P, c0 : c0 + n_tiles * P], in_=res[:])
-
         open_acc = {}
 
         def run_pass(item):
-            first, n_tiles, codes, scales, m, gp, on_vector = item
+            gi, first, n_tiles, codes, scales, m, gp = item
             width = n_tiles * P
             if gp == 0:
-                open_acc[m] = accs.tile([P, width], F32, name="acc", tag="acc")
+                if gi == LAST and m >= 2:
+                    spare = banks.tile([P, 512], F32, name="bank", tag="bank")
+                    open_acc[m] = spare[:, :width]
+                else:
+                    acc_tile = accs.tile([P, width], F32, name="acc", tag="acc")
+                    open_acc[m] = acc_tile[:, :]
             acc = open_acc[m]
             xw = ((m // 2) * 2 * PASSES + gp * 2 + m % 2) * P
             xc = slice(xw, xw + P)
             wc = slice(gp * width, (gp + 1) * width)
             nc.tensor.matmul_mx(
-                out=acc[:],
+                out=acc,
                 lhsT=x_codes[:, xc].bitcast(FP8X4),
                 lhsT_scale=x_scales[:, xc],
                 rhs=codes[:, wc].bitcast(FP8X4),
@@ -274,7 +276,7 @@ def tile_selfattention_pa_kernel(tc, x, freqs, w_bytes, w_scale, b, g, out):
                 stop=(gp == PASSES - 1),
             )
             if gp == PASSES - 1:
-                epilogue(first, n_tiles, m, acc, on_vector)
+                project(gi, first, n_tiles, m, acc)
 
         todo = []
         st = {"done": 0, "first": 0}
@@ -282,7 +284,10 @@ def tile_selfattention_pa_kernel(tc, x, freqs, w_bytes, w_scale, b, g, out):
         def run_group(gi):
             n_tiles = GROUP_TILES[gi]
             first = st["first"]
+            last = gi == LAST
             grp = grouped.tile([P, PASSES * n_tiles * 512], BF16, name="grp", tag="grp", align_bytes=64)
+            codes = wq.tile([P, PASSES * n_tiles * P], U32, name="w_codes", tag="w_codes", align_bytes=64)
+            scales = wq.tile([P, PASSES * n_tiles * P], U8, name="w_scales", tag="w_scales", align_bytes=64)
             stops = (1, 4, 7, 10) if n_tiles == 4 else (1, 4)
             slots = len(stops)
             for r in range(0, n_tiles, 2):
@@ -297,10 +302,7 @@ def tile_selfattention_pa_kernel(tc, x, freqs, w_bytes, w_scale, b, g, out):
                     if gp % 2 == 0 and i + 2 < ROW_TILES:
                         cast_cols(i + 2, st["two_next"], gp * 512, gp * 512 + 1024)
                     bank = transpose_pass(two, gp)
-                    if (gi % 2 == 1 or gi == len(GROUP_TILES) - 1) and r == n_tiles - 2 and gp == 0:
-                        scale_out_scalar(bank, grp, n_tiles, r, gp)
-                    else:
-                        scale_out(bank, grp, n_tiles, r, gp)
+                    scale_out(bank, grp, n_tiles, r, gp)
                     if (r // 2) * PASSES + gp in stops:
                         share = -((st["done"] - len(todo)) // slots)
                         for item in todo[st["done"] : st["done"] + share]:
@@ -313,14 +315,11 @@ def tile_selfattention_pa_kernel(tc, x, freqs, w_bytes, w_scale, b, g, out):
                         tables_first_turn()
                     else:
                         tables_second_turn()
-            codes = wq.tile([P, PASSES * n_tiles * P], U32, name="w_codes", tag="w_codes", align_bytes=64)
-            scales = wq.tile([P, PASSES * n_tiles * P], U8, name="w_scales", tag="w_scales", align_bytes=64)
-            quantize(grp, codes, scales, 0)
+            quantize(grp, 0, PASSES * n_tiles * 512, codes, scales, 0)
             release_held(codes)
-            last = gi == len(GROUP_TILES) - 1
             for m in range(M_TILES):
                 for gp in range(PASSES):
-                    todo.append((first, n_tiles, codes, scales, m, gp, last and m != 1))
+                    todo.append((gi, first, n_tiles, codes, scales, m, gp))
             st["first"] = first + n_tiles
 
         with tc.manual_schedule(engines={mybir.EngineType.PE}):
@@ -333,4 +332,5 @@ def tile_selfattention_pa_kernel(tc, x, freqs, w_bytes, w_scale, b, g, out):
                 run_group(gi)
             for item in todo[st["done"] :]:
                 run_pass(item)
-            finish()
+            while finished[0] < len(waiting):
+                finish()

@@ -54,8 +54,9 @@ def tile_selfattention_pa_kernel(tc, x, freqs, w_bytes, w_scale, b, g, out):
         proj = ctx.enter_context(tc.tile_pool(name="proj", bufs=7))
         epi = ctx.enter_context(tc.tile_pool(name="epi", bufs=6))
         small = ctx.enter_context(tc.tile_pool(name="small", bufs=8))
-        banks = ctx.enter_context(tc.psum_pool(name="banks", bufs=5))
+        banks = ctx.enter_context(tc.psum_pool(name="banks", bufs=4))
         tabs = ctx.enter_context(tc.psum_pool(name="tabs", bufs=1))
+        sums = ctx.enter_context(tc.psum_pool(name="sums", bufs=1))
         accs = ctx.enter_context(tc.psum_pool(name="accs", bufs=2))
 
         k_scale = const.tile([P, PASSES, 4], F32, name="k_scale")
@@ -180,6 +181,15 @@ def tile_selfattention_pa_kernel(tc, x, freqs, w_bytes, w_scale, b, g, out):
                 op=ALU.mult,
             )
 
+        def scale_out_scalar(bank, grp, n_tiles, r, gp):
+            col = (gp * n_tiles + r) * 512
+            dst = grp[:, col : col + 1024].rearrange("p (n t) -> p n t", t=4)
+            srcv = bank[:].bitcast(BF16).rearrange("p (u n e) -> p n u e", u=2, e=2)
+            for u in (0, 1):
+                for e in (0, 1):
+                    t = 2 * u + e
+                    nc.scalar.activation(out=dst[:, :, t], in_=srcv[:, :, u, e], func=ACT.Copy, scale=k_scale[:, gp, t : t + 1])
+
         waiting = []
         finished = [0]
         held = []
@@ -199,12 +209,17 @@ def tile_selfattention_pa_kernel(tc, x, freqs, w_bytes, w_scale, b, g, out):
             rinv = small.tile([P, n_tiles], F32, name="rinv", tag="rinv")
             nc.scalar.activation(out=rinv[:], in_=ss[:], func=ACT.Abs_reciprocal_sqrt, bias=EPS, scale=1.0 / HEAD)
             unit = (gi, pr, rinv, n_tiles, m, c0)
-            rotate(unit)
+            if m == 3 and gi < 4:
+                held_all.append(unit)
+            else:
+                rotate(unit)
+
+        held_all = []
 
         def rotate(unit):
             gi, pr, rinv, n_tiles, m, c0 = unit
             last = gi == LAST
-            helped = m == 3 or (m == 2 and gi >= 4)
+            helped = m == 3 and gi >= 4
             eng = nc.vector if last and m != 1 else nc.gpsimd
             shape4 = [P, n_tiles, HEAD // 2, 2]
             pv = pr[:].rearrange("p (h j l) -> p h j l", h=n_tiles, l=2)
@@ -220,10 +235,24 @@ def tile_selfattention_pa_kernel(tc, x, freqs, w_bytes, w_scale, b, g, out):
                 )
                 terms.append(t)
             unit = (eng, terms, rinv, n_tiles, m, c0)
-            if m == 3 and not last:
+            if m == 3 and gi < 4:
+                to_sum.append((st["stop"] + (1), terms, rinv, n_tiles, m, c0))
+            elif m == 3 and gi >= 4 and not last:
                 held.append(unit)
             else:
                 add_terms(unit)
+
+        to_sum = []
+
+        def sum_on_tensor():
+            due, terms, rinv, n_tiles, m, c0 = to_sum[0]
+            to_sum.remove(to_sum[0])
+            total = sums.tile([P, 512], F32, name="total", tag="total")
+            for l in (0, 1):
+                nc.tensor.matmul(
+                    out=total[:, : n_tiles * P], lhsT=ident[:], rhs=terms[l][:], start=(l == 0), stop=(l == 1)
+                )
+            close(total, terms[0], rinv, n_tiles, m, c0)
 
         def add_terms(unit):
             eng, terms, rinv, n_tiles, m, c0 = unit
@@ -244,11 +273,15 @@ def tile_selfattention_pa_kernel(tc, x, freqs, w_bytes, w_scale, b, g, out):
             nc.sync.dma_start(out=out_rows[m * P : (m + 1) * P, c0 : c0 + n_tiles * P], in_=res[:])
 
         def release_held(codes):
-            if held:
+            if held or held_all:
                 seen = small.tile([P, 1], U32, name="seen", tag="seen")
                 nc.gpsimd.tensor_copy(out=seen[:], in_=codes[:, codes.shape[1] - 1 :])
-                add_terms(held[0])
+                for unit in held:
+                    add_terms(unit)
                 held.clear()
+                for unit in held_all:
+                    rotate(unit)
+                held_all.clear()
 
         open_acc = {}
 
@@ -279,7 +312,7 @@ def tile_selfattention_pa_kernel(tc, x, freqs, w_bytes, w_scale, b, g, out):
                 project(gi, first, n_tiles, m, acc)
 
         todo = []
-        st = {"done": 0, "first": 0}
+        st = {"done": 0, "first": 0, "stop": 0}
 
         def run_group(gi):
             n_tiles = GROUP_TILES[gi]
@@ -302,13 +335,20 @@ def tile_selfattention_pa_kernel(tc, x, freqs, w_bytes, w_scale, b, g, out):
                     if gp % 2 == 0 and i + 2 < ROW_TILES:
                         cast_cols(i + 2, st["two_next"], gp * 512, gp * 512 + 1024)
                     bank = transpose_pass(two, gp)
-                    scale_out(bank, grp, n_tiles, r, gp)
+                    if (gi % 2 == 1 or gi == LAST) and r == n_tiles - 2 and gp == 0:
+                        scale_out_scalar(bank, grp, n_tiles, r, gp)
+                    else:
+                        scale_out(bank, grp, n_tiles, r, gp)
                     if (r // 2) * PASSES + gp in stops:
+                        ready_sums = len([q for q in to_sum if q[0] <= st["stop"]])
+                        st["stop"] += 1
                         share = -((st["done"] - len(todo)) // slots)
                         for item in todo[st["done"] : st["done"] + share]:
                             run_pass(item)
                         st["done"] += share
                         slots -= 1
+                        for q in range(ready_sums):
+                            sum_on_tensor()
                 if i < M_TILES:
                     x_stage(i // 2)
                     if i == 0:
@@ -325,12 +365,17 @@ def tile_selfattention_pa_kernel(tc, x, freqs, w_bytes, w_scale, b, g, out):
         with tc.manual_schedule(engines={mybir.EngineType.PE}):
             st["two_next"] = new_pair()
             for c0 in range(0, K, 512):
-                cast_cols(0, st["two_next"], c0, c0 + 512)
+                first_pair = st["two_next"]
+                nc.scalar.copy(out=first_pair[0][:, c0 : c0 + 512], in_=wb_tiles[0][:, c0 : c0 + 512].bitcast(FP8))
+                caster = nc.vector.tensor_copy if c0 < 1 * 512 else nc.scalar.copy
+                caster(out=first_pair[1][:, c0 : c0 + 512], in_=wb_tiles[1][:, c0 : c0 + 512].bitcast(FP8))
             run_group(0)
         with tc.manual_schedule(engines={mybir.EngineType.PE, mybir.EngineType.Activation, mybir.EngineType.Pool}):
             for gi in range(1, len(GROUP_TILES)):
                 run_group(gi)
             for item in todo[st["done"] :]:
                 run_pass(item)
+            while to_sum:
+                sum_on_tensor()
             while finished[0] < len(waiting):
                 finish()

@@ -102,18 +102,16 @@ def tile_selfattention_pa_kernel(tc, x, freqs, w_bytes, w_scale, b, g, out):
         b_bc = const.tile([P, CHANNELS], BF16, name="b_bc")
         nc.sync.dma_start(out=b_bc[:], in_=b.partition_broadcast(P))
 
-        rot = []
+        rot = const.tile([P, M_TILES, 2 * HEAD], F32, name="rot")
         fr_v = fr_sb[:].rearrange("p m (j i l) -> p m j i l", i=2, l=2)
         g_v = g_bc[:].rearrange("p (j l) -> p j l", l=2)
         for l in (0, 1):
-            rl = const.tile([P, M_TILES, HEAD], F32, name="rot%d" % l)
             nc.gpsimd.tensor_tensor(
-                out=rl[:].rearrange("p m (j i) -> p m j i", i=2),
+                out=rot[:, :, l * HEAD : (l + 1) * HEAD].rearrange("p m (j i) -> p m j i", i=2),
                 in0=fr_v[:, :, :, :, l],
                 in1=g_v[:, :, l].unsqueeze(1).unsqueeze(3).to_broadcast([P, M_TILES, HEAD // 2, 2]),
                 op=ALU.mult,
             )
-            rot.append(rl)
 
         rot_turned = const.tile([P, 4 * HEAD], F32, name="rot_turned")
         rot_ps = tabs.tile([P, 4 * HEAD], F32, name="rot_ps")
@@ -123,7 +121,7 @@ def tile_selfattention_pa_kernel(tc, x, freqs, w_bytes, w_scale, b, g, out):
             for m in (2, 3):
                 for l in (0, 1):
                     col = (2 * (m - 2) + l) * HEAD
-                    nc.tensor.transpose(out=bank[:, col : col + HEAD], in_=rot[l][:, m, :], identity=ident[:])
+                    nc.tensor.transpose(out=bank[:, col : col + HEAD], in_=rot[:, m, l * HEAD : (l + 1) * HEAD], identity=ident[:])
             nc.vector.tensor_copy(out=rot_turned[:], in_=bank[:])
 
         def tables_second_turn():
@@ -181,15 +179,6 @@ def tile_selfattention_pa_kernel(tc, x, freqs, w_bytes, w_scale, b, g, out):
                 op=ALU.mult,
             )
 
-        def scale_out_scalar(bank, grp, n_tiles, r, gp):
-            col = (gp * n_tiles + r) * 512
-            dst = grp[:, col : col + 1024].rearrange("p (n t) -> p n t", t=4)
-            srcv = bank[:].bitcast(BF16).rearrange("p (u n e) -> p n u e", u=2, e=2)
-            for u in (0, 1):
-                for e in (0, 1):
-                    t = 2 * u + e
-                    nc.scalar.activation(out=dst[:, :, t], in_=srcv[:, :, u, e], func=ACT.Copy, scale=k_scale[:, gp, t : t + 1])
-
         waiting = []
         finished = [0]
         held = []
@@ -219,21 +208,18 @@ def tile_selfattention_pa_kernel(tc, x, freqs, w_bytes, w_scale, b, g, out):
         def rotate(unit):
             gi, pr, rinv, n_tiles, m, c0 = unit
             last = gi == LAST
-            helped = m == 3 and gi >= 4
+            helped = (m >= 2 and gi >= 4)
             eng = nc.vector if last and m != 1 else nc.gpsimd
-            shape4 = [P, n_tiles, HEAD // 2, 2]
-            pv = pr[:].rearrange("p (h j l) -> p h j l", h=n_tiles, l=2)
-            terms = []
-            for l in (0, 1):
-                t = epi.tile([P, n_tiles * P], F32, name="term%d" % l, tag="term%d" % l)
-                table = rot_ps[:, (2 * (m - 2) + l) * HEAD : (2 * (m - 2) + l + 1) * HEAD] if helped else rot[l][:, m, :]
-                (nc.vector if helped else eng).tensor_tensor(
-                    out=t[:].rearrange("p (h j i) -> p h j i", h=n_tiles, i=2),
-                    in0=pv[:, :, :, l : l + 1].to_broadcast(shape4),
-                    in1=table.rearrange("p (j i) -> p j i", i=2).unsqueeze(1).to_broadcast(shape4),
-                    op=ALU.mult,
-                )
-                terms.append(t)
+            width = n_tiles * P
+            shape5 = [P, 2, n_tiles, HEAD // 2, 2]
+            terms = epi.tile([P, 2, width], F32, name="terms", tag="terms")
+            table = rot_ps[:, 2 * (m - 2) * HEAD : 2 * (m - 1) * HEAD] if helped else rot[:, m, :]
+            (nc.vector if helped else eng).tensor_tensor(
+                out=terms[:].rearrange("p l (h j i) -> p l h j i", h=n_tiles, i=2),
+                in0=pr[:].rearrange("p (h j l) -> p l h j", h=n_tiles, l=2).unsqueeze(4).to_broadcast(shape5),
+                in1=table.rearrange("p (l j i) -> p l j i", l=2, i=2).unsqueeze(2).to_broadcast(shape5),
+                op=ALU.mult,
+            )
             unit = (eng, terms, rinv, n_tiles, m, c0)
             if m == 3 and gi < 4:
                 to_sum.append((st["stop"] + (1), terms, rinv, n_tiles, m, c0))
@@ -250,14 +236,14 @@ def tile_selfattention_pa_kernel(tc, x, freqs, w_bytes, w_scale, b, g, out):
             total = sums.tile([P, 512], F32, name="total", tag="total")
             for l in (0, 1):
                 nc.tensor.matmul(
-                    out=total[:, : n_tiles * P], lhsT=ident[:], rhs=terms[l][:], start=(l == 0), stop=(l == 1)
+                    out=total[:, : n_tiles * P], lhsT=ident[:], rhs=terms[:, l, :], start=(l == 0), stop=(l == 1)
                 )
-            close(total, terms[0], rinv, n_tiles, m, c0)
+            close(total[:], terms[:, 0, :], rinv, n_tiles, m, c0)
 
         def add_terms(unit):
             eng, terms, rinv, n_tiles, m, c0 = unit
-            eng.tensor_tensor(out=terms[0][:], in0=terms[0][:], in1=terms[1][:], op=ALU.add)
-            close(terms[0], terms[0], rinv, n_tiles, m, c0)
+            eng.tensor_tensor(out=terms[:, 0, :], in0=terms[:, 0, :], in1=terms[:, 1, :], op=ALU.add)
+            close(terms[:, 0, :], terms[:, 0, :], rinv, n_tiles, m, c0)
 
         def close(src, res, rinv, n_tiles, m, c0):
             waiting.append((src, res, rinv, n_tiles, m, c0))
@@ -270,7 +256,7 @@ def tile_selfattention_pa_kernel(tc, x, freqs, w_bytes, w_scale, b, g, out):
             for h in range(n_tiles):
                 cols = slice(h * HEAD, (h + 1) * HEAD)
                 nc.scalar.activation(out=res[:, cols], in_=src[:, cols], func=ACT.Copy, scale=rinv[:, h : h + 1])
-            nc.sync.dma_start(out=out_rows[m * P : (m + 1) * P, c0 : c0 + n_tiles * P], in_=res[:])
+            nc.sync.dma_start(out=out_rows[m * P : (m + 1) * P, c0 : c0 + n_tiles * P], in_=res)
 
         def release_held(codes):
             if held or held_all:
@@ -335,10 +321,10 @@ def tile_selfattention_pa_kernel(tc, x, freqs, w_bytes, w_scale, b, g, out):
                     if gp % 2 == 0 and i + 2 < ROW_TILES:
                         cast_cols(i + 2, st["two_next"], gp * 512, gp * 512 + 1024)
                     bank = transpose_pass(two, gp)
-                    if (gi % 2 == 1 or gi == LAST) and r == n_tiles - 2 and gp == 0:
-                        scale_out_scalar(bank, grp, n_tiles, r, gp)
-                    else:
-                        scale_out(bank, grp, n_tiles, r, gp)
+                    scale_out(bank, grp, n_tiles, r, gp)
+                    if last and gp in (3, PASSES - 1):
+                        done = 0 if gp == 3 else 4
+                        quantize(grp, done * n_tiles * 512, (gp + 1 - done) * n_tiles * 512, codes, scales, done * n_tiles * P)
                     if (r // 2) * PASSES + gp in stops:
                         ready_sums = len([q for q in to_sum if q[0] <= st["stop"]])
                         st["stop"] += 1
@@ -355,11 +341,13 @@ def tile_selfattention_pa_kernel(tc, x, freqs, w_bytes, w_scale, b, g, out):
                         tables_first_turn()
                     else:
                         tables_second_turn()
-            quantize(grp, 0, PASSES * n_tiles * 512, codes, scales, 0)
+            if not last:
+                quantize(grp, 0, PASSES * n_tiles * 512, codes, scales, 0)
             release_held(codes)
-            for m in range(M_TILES):
-                for gp in range(PASSES):
-                    todo.append((gi, first, n_tiles, codes, scales, m, gp))
+            for gps in (range(4), range(4, PASSES)) if last else (range(PASSES),):
+                for m in range(M_TILES):
+                    for gp in gps:
+                        todo.append((gi, first, n_tiles, codes, scales, m, gp))
             st["first"] = first + n_tiles
 
         with tc.manual_schedule(engines={mybir.EngineType.PE}):

@@ -54,9 +54,8 @@ def tile_selfattention_pa_kernel(tc, x, freqs, w_bytes, w_scale, b, g, out):
         proj = ctx.enter_context(tc.tile_pool(name="proj", bufs=7))
         epi = ctx.enter_context(tc.tile_pool(name="epi", bufs=6))
         small = ctx.enter_context(tc.tile_pool(name="small", bufs=8))
-        banks = ctx.enter_context(tc.psum_pool(name="banks", bufs=4))
+        banks = ctx.enter_context(tc.psum_pool(name="banks", bufs=5))
         tabs = ctx.enter_context(tc.psum_pool(name="tabs", bufs=1))
-        sums = ctx.enter_context(tc.psum_pool(name="sums", bufs=1))
         accs = ctx.enter_context(tc.psum_pool(name="accs", bufs=2))
 
         k_scale = const.tile([P, PASSES, 4], F32, name="k_scale")
@@ -156,7 +155,7 @@ def tile_selfattention_pa_kernel(tc, x, freqs, w_bytes, w_scale, b, g, out):
             gx = grouped.tile([P, 2 * K], BF16, name="gx", tag="gx", bufs=1, align_bytes=64)
             for gp in range(PASSES):
                 bank = transpose_pass(two, gp)
-                mover = nc.vector.tensor_copy if mp == 0 else nc.scalar.copy
+                mover = nc.vector.tensor_copy if mp == 0 and gp < 4 else nc.scalar.copy
                 mover(
                     out=gx[:, gp * 1024 : (gp + 1) * 1024].bitcast(F32).rearrange("p (n u) -> p n u", u=2),
                     in_=bank[:].rearrange("p (u n) -> p n u", u=2),
@@ -178,6 +177,15 @@ def tile_selfattention_pa_kernel(tc, x, freqs, w_bytes, w_scale, b, g, out):
                 in1=k_scale[:, gp, :].rearrange("p (u e) -> p u e", e=2).unsqueeze(1).to_broadcast([P, 2 * P, 2, 2]),
                 op=ALU.mult,
             )
+
+        def scale_out_scalar(bank, grp, n_tiles, r, gp):
+            col = (gp * n_tiles + r) * 512
+            dst = grp[:, col : col + 1024].rearrange("p (n t) -> p n t", t=4)
+            srcv = bank[:].bitcast(BF16).rearrange("p (u n e) -> p n u e", u=2, e=2)
+            for u in (0, 1):
+                for e in (0, 1):
+                    t = 2 * u + e
+                    nc.scalar.activation(out=dst[:, :, t], in_=srcv[:, :, u, e], func=ACT.Copy, scale=k_scale[:, gp, t : t + 1])
 
         waiting = []
         finished = [0]
@@ -221,24 +229,10 @@ def tile_selfattention_pa_kernel(tc, x, freqs, w_bytes, w_scale, b, g, out):
                 op=ALU.mult,
             )
             unit = (eng, terms, rinv, n_tiles, m, c0)
-            if m == 3 and gi < 4:
-                to_sum.append((st["stop"] + (1), terms, rinv, n_tiles, m, c0))
-            elif m == 3 and gi >= 4 and not last:
+            if m == 3 and gi >= 4 and not last:
                 held.append(unit)
             else:
                 add_terms(unit)
-
-        to_sum = []
-
-        def sum_on_tensor():
-            due, terms, rinv, n_tiles, m, c0 = to_sum[0]
-            to_sum.remove(to_sum[0])
-            total = sums.tile([P, 512], F32, name="total", tag="total")
-            for l in (0, 1):
-                nc.tensor.matmul(
-                    out=total[:, : n_tiles * P], lhsT=ident[:], rhs=terms[:, l, :], start=(l == 0), stop=(l == 1)
-                )
-            close(total[:], terms[:, 0, :], rinv, n_tiles, m, c0)
 
         def add_terms(unit):
             eng, terms, rinv, n_tiles, m, c0 = unit
@@ -298,7 +292,7 @@ def tile_selfattention_pa_kernel(tc, x, freqs, w_bytes, w_scale, b, g, out):
                 project(gi, first, n_tiles, m, acc)
 
         todo = []
-        st = {"done": 0, "first": 0, "stop": 0}
+        st = {"done": 0, "first": 0}
 
         def run_group(gi):
             n_tiles = GROUP_TILES[gi]
@@ -321,33 +315,27 @@ def tile_selfattention_pa_kernel(tc, x, freqs, w_bytes, w_scale, b, g, out):
                     if gp % 2 == 0 and i + 2 < ROW_TILES:
                         cast_cols(i + 2, st["two_next"], gp * 512, gp * 512 + 1024)
                     bank = transpose_pass(two, gp)
-                    scale_out(bank, grp, n_tiles, r, gp)
-                    if last and gp in (3, PASSES - 1):
-                        done = 0 if gp == 3 else 4
-                        quantize(grp, done * n_tiles * 512, (gp + 1 - done) * n_tiles * 512, codes, scales, done * n_tiles * P)
+                    if gi == LAST and gp == 1:
+                        scale_out_scalar(bank, grp, n_tiles, r, gp)
+                    else:
+                        scale_out(bank, grp, n_tiles, r, gp)
                     if (r // 2) * PASSES + gp in stops:
-                        ready_sums = len([q for q in to_sum if q[0] <= st["stop"]])
-                        st["stop"] += 1
                         share = -((st["done"] - len(todo)) // slots)
                         for item in todo[st["done"] : st["done"] + share]:
                             run_pass(item)
                         st["done"] += share
                         slots -= 1
-                        for q in range(ready_sums):
-                            sum_on_tensor()
                 if i < M_TILES:
                     x_stage(i // 2)
                     if i == 0:
                         tables_first_turn()
                     else:
                         tables_second_turn()
-            if not last:
-                quantize(grp, 0, PASSES * n_tiles * 512, codes, scales, 0)
+            quantize(grp, 0, PASSES * n_tiles * 512, codes, scales, 0)
             release_held(codes)
-            for gps in (range(4), range(4, PASSES)) if last else (range(PASSES),):
-                for m in range(M_TILES):
-                    for gp in gps:
-                        todo.append((gi, first, n_tiles, codes, scales, m, gp))
+            for m in range(M_TILES):
+                for gp in range(PASSES):
+                    todo.append((gi, first, n_tiles, codes, scales, m, gp))
             st["first"] = first + n_tiles
 
         with tc.manual_schedule(engines={mybir.EngineType.PE}):
@@ -363,7 +351,5 @@ def tile_selfattention_pa_kernel(tc, x, freqs, w_bytes, w_scale, b, g, out):
                 run_group(gi)
             for item in todo[st["done"] :]:
                 run_pass(item)
-            while to_sum:
-                sum_on_tensor()
             while finished[0] < len(waiting):
                 finish()

@@ -301,7 +301,7 @@ def tile_selfattention_pa_kernel(tc, x, freqs, w_bytes, w_scale, b, g, out):
             grp = grouped.tile([P, PASSES * n_tiles * 512], BF16, name="grp", tag="grp", align_bytes=64)
             codes = wq.tile([P, PASSES * n_tiles * P], U32, name="w_codes", tag="w_codes", align_bytes=64)
             scales = wq.tile([P, PASSES * n_tiles * P], U8, name="w_scales", tag="w_scales", align_bytes=64)
-            stops = (1, 4, 7, 10) if n_tiles == 4 else (1, 4)
+            stops = (1, 4, 7, 10) if n_tiles == 4 else (2, 4)
             slots = len(stops)
             for r in range(0, n_tiles, 2):
                 i = first + r
@@ -315,10 +315,13 @@ def tile_selfattention_pa_kernel(tc, x, freqs, w_bytes, w_scale, b, g, out):
                     if gp % 2 == 0 and i + 2 < ROW_TILES:
                         cast_cols(i + 2, st["two_next"], gp * 512, gp * 512 + 1024)
                     bank = transpose_pass(two, gp)
-                    if gi == LAST and gp == 1:
+                    if gi in (1, 3) and r == 0 and gp == 0 or gi == 6 and gp == 1:
                         scale_out_scalar(bank, grp, n_tiles, r, gp)
                     else:
                         scale_out(bank, grp, n_tiles, r, gp)
+                    if last and gp in (3, PASSES - 1):
+                        done = 0 if gp == 3 else 4
+                        quantize(grp, done * n_tiles * 512, (gp + 1 - done) * n_tiles * 512, codes, scales, done * n_tiles * P)
                     if (r // 2) * PASSES + gp in stops:
                         share = -((st["done"] - len(todo)) // slots)
                         for item in todo[st["done"] : st["done"] + share]:
@@ -331,11 +334,13 @@ def tile_selfattention_pa_kernel(tc, x, freqs, w_bytes, w_scale, b, g, out):
                         tables_first_turn()
                     else:
                         tables_second_turn()
-            quantize(grp, 0, PASSES * n_tiles * 512, codes, scales, 0)
+            if not last:
+                quantize(grp, 0, PASSES * n_tiles * 512, codes, scales, 0)
             release_held(codes)
-            for m in range(M_TILES):
-                for gp in range(PASSES):
-                    todo.append((gi, first, n_tiles, codes, scales, m, gp))
+            for gps in (range(4), range(4, PASSES)) if last else (range(PASSES),):
+                for m in range(M_TILES):
+                    for gp in gps:
+                        todo.append((gi, first, n_tiles, codes, scales, m, gp))
             st["first"] = first + n_tiles
 
         with tc.manual_schedule(engines={mybir.EngineType.PE}):

@@ -265,6 +265,12 @@ def tile_selfattention_pa_kernel(tc, x, freqs, w_bytes, w_scale, b, g, out):
 
         open_acc = {}
 
+        def warm_up(src, count):
+            acc_tile = accs.tile([P, 512], F32, name="acc", tag="acc")
+            end = src.shape[1]
+            for q in range(count):
+                nc.tensor.matmul(out=acc_tile[:], lhsT=src[:, end - P :], rhs=src[:, end - 512 :], start=True, stop=True)
+
         def run_pass(item):
             gi, first, n_tiles, codes, scales, m, gp = item
             width = n_tiles * P
@@ -292,16 +298,17 @@ def tile_selfattention_pa_kernel(tc, x, freqs, w_bytes, w_scale, b, g, out):
                 project(gi, first, n_tiles, m, acc)
 
         todo = []
-        st = {"done": 0, "first": 0}
+        st = {"done": 0, "first": 0, "grp": None}
 
         def run_group(gi):
             n_tiles = GROUP_TILES[gi]
             first = st["first"]
             last = gi == LAST
+            before = st["grp"]
             grp = grouped.tile([P, PASSES * n_tiles * 512], BF16, name="grp", tag="grp", align_bytes=64)
             codes = wq.tile([P, PASSES * n_tiles * P], U32, name="w_codes", tag="w_codes", align_bytes=64)
             scales = wq.tile([P, PASSES * n_tiles * P], U8, name="w_scales", tag="w_scales", align_bytes=64)
-            stops = (1, 4, 7, 10) if n_tiles == 4 else (2, 4)
+            stops = (1,2,4,5,7,8,10,11) if n_tiles == 4 else (2, 4)
             slots = len(stops)
             for r in range(0, n_tiles, 2):
                 i = first + r
@@ -323,6 +330,8 @@ def tile_selfattention_pa_kernel(tc, x, freqs, w_bytes, w_scale, b, g, out):
                         done = 0 if gp == 3 else 4
                         quantize(grp, done * n_tiles * 512, (gp + 1 - done) * n_tiles * 512, codes, scales, done * n_tiles * P)
                     if (r // 2) * PASSES + gp in stops:
+                        if gi > 0 and slots == len(stops):
+                            warm_up(before, 2)
                         share = -((st["done"] - len(todo)) // slots)
                         for item in todo[st["done"] : st["done"] + share]:
                             run_pass(item)
@@ -342,6 +351,7 @@ def tile_selfattention_pa_kernel(tc, x, freqs, w_bytes, w_scale, b, g, out):
                     for gp in gps:
                         todo.append((gi, first, n_tiles, codes, scales, m, gp))
             st["first"] = first + n_tiles
+            st["grp"] = grp
 
         with tc.manual_schedule(engines={mybir.EngineType.PE}):
             st["two_next"] = new_pair()

@@ -178,6 +178,18 @@ def tile_selfattention_pa_kernel(tc, x, freqs, w_bytes, w_scale, b, g, out):
                 op=ALU.mult,
             )
 
+        def scale_in_place(bank, grp, n_tiles, r, gp):
+            col = (gp * n_tiles + r) * 512
+            nc.scalar.copy(
+                out=grp[:, col : col + 1024].bitcast(F32).rearrange("p (n u) -> p n u", u=2),
+                in_=bank[:].rearrange("p (u n) -> p n u", u=2),
+            )
+            for a in range(col, col + 1024, 1024):
+                values = grp[:, a : a + 1024].rearrange("p (n t) -> p n t", t=4)
+                nc.gpsimd.tensor_tensor(
+                    out=values, in0=values, in1=k_scale[:, gp, :].unsqueeze(1).to_broadcast([P, 256, 4]), op=ALU.mult
+                )
+
         def scale_out_scalar(bank, grp, n_tiles, r, gp):
             col = (gp * n_tiles + r) * 512
             dst = grp[:, col : col + 1024].rearrange("p (n t) -> p n t", t=4)
@@ -206,12 +218,15 @@ def tile_selfattention_pa_kernel(tc, x, freqs, w_bytes, w_scale, b, g, out):
             rinv = small.tile([P, n_tiles], F32, name="rinv", tag="rinv")
             nc.scalar.activation(out=rinv[:], in_=ss[:], func=ACT.Abs_reciprocal_sqrt, bias=EPS, scale=1.0 / HEAD)
             unit = (gi, pr, rinv, n_tiles, m, c0)
-            if m == 3 and gi < 4:
+            if last:
+                last_units.append(unit)
+            elif m == 3 and gi < 4:
                 held_all.append(unit)
             else:
                 rotate(unit)
 
         held_all = []
+        last_units = []
 
         def rotate(unit):
             gi, pr, rinv, n_tiles, m, c0 = unit
@@ -322,7 +337,9 @@ def tile_selfattention_pa_kernel(tc, x, freqs, w_bytes, w_scale, b, g, out):
                     if gp % 2 == 0 and i + 2 < ROW_TILES:
                         cast_cols(i + 2, st["two_next"], gp * 512, gp * 512 + 1024)
                     bank = transpose_pass(two, gp)
-                    if gi in (1, 3) and r == 0 and gp == 0 or gi == 6 and gp == 1:
+                    if gi == 6 and gp == 0:
+                        scale_in_place(bank, grp, n_tiles, r, gp)
+                    elif gi in (1, 3) and r == 0 and gp == 0 or gi == 6 and gp == 1:
                         scale_out_scalar(bank, grp, n_tiles, r, gp)
                     else:
                         scale_out(bank, grp, n_tiles, r, gp)
@@ -364,7 +381,12 @@ def tile_selfattention_pa_kernel(tc, x, freqs, w_bytes, w_scale, b, g, out):
         with tc.manual_schedule(engines={mybir.EngineType.PE, mybir.EngineType.Activation, mybir.EngineType.Pool}):
             for gi in range(1, len(GROUP_TILES)):
                 run_group(gi)
+        with tc.manual_schedule(
+            engines={mybir.EngineType.PE, mybir.EngineType.Activation, mybir.EngineType.Pool, mybir.EngineType.DVE}
+        ):
             for item in todo[st["done"] :]:
                 run_pass(item)
+            for m in (1, 2, 3, 0):
+                rotate(last_units[m])
             while finished[0] < len(waiting):
                 finish()

from contextlib import ExitStack

import concourse.mybir as mybir
from concourse.masks import make_identity

F32 = mybir.dt.float32
BF16 = mybir.dt.bfloat16
U32 = mybir.dt.uint32
U8 = mybir.dt.uint8
FP8 = mybir.dt.float8_e4m3fn
FP8X4 = mybir.dt.float8_e4m3fn_x4
ACT = mybir.ActivationFunctionType
ALU = mybir.AluOpType

P = 128
K = 3072
TOKENS = 512
CHANNELS = 3072
HEAD = 128
EPS = 1e-6
PASSES = K // 512
M_TILES = TOKENS // P
ROW_TILES = CHANNELS // P
GROUP_TILES = (4, 4, 4, 4, 4, 2, 2)
LAST = len(GROUP_TILES) - 1
PREFETCH = 6

FLOPS = 2 * TOKENS * K * CHANNELS


def quantize_widths(total):
    widths = []
    while total > 0:
        w = 4096
        while w > total:
            w //= 2
        widths.append(w)
        total -= w
    return widths


def tile_selfattention_pa_kernel(tc, x, freqs, w_bytes, w_scale, b, g, out):
    nc = tc.nc
    x_rows = x.rearrange("o s k -> (o s) k")
    out_rows = out.rearrange("o s h d -> (o s) (h d)")
    fr_rows = freqs.rearrange("o s a j i l -> (o s a) (j i l)")

    with ExitStack() as ctx:
        const = ctx.enter_context(tc.tile_pool(name="const", bufs=1))
        wbytes = ctx.enter_context(tc.tile_pool(name="wbytes", bufs=PREFETCH + 2))
        rows = ctx.enter_context(tc.tile_pool(name="rows", bufs=8))
        grouped = ctx.enter_context(tc.tile_pool(name="grouped", bufs=2))
        wq = ctx.enter_context(tc.tile_pool(name="wq", bufs=2))
        proj = ctx.enter_context(tc.tile_pool(name="proj", bufs=7))
        epi = ctx.enter_context(tc.tile_pool(name="epi", bufs=6))
        small = ctx.enter_context(tc.tile_pool(name="small", bufs=8))
        banks = ctx.enter_context(tc.psum_pool(name="banks", bufs=5))
        tabs = ctx.enter_context(tc.psum_pool(name="tabs", bufs=1))
        accs = ctx.enter_context(tc.psum_pool(name="accs", bufs=2))

        k_scale = const.tile([P, PASSES, 4], F32, name="k_scale")
        nc.scalar.dma_start(out=k_scale[:], in_=w_scale.rearrange("o (g p t) -> p (o g) t", p=P, t=4))
        fr_sb = const.tile([P, M_TILES, 256], BF16, name="fr_sb")
        nc.scalar.dma_start(out=fr_sb[:], in_=fr_rows.rearrange("(m p) c -> p m c", p=P))
        g_bc = const.tile([P, HEAD], BF16, name="g_bc")
        nc.scalar.dma_start(out=g_bc[:], in_=g.partition_broadcast(P))

        one = const.tile([P, 1], F32, name="one")
        nc.gpsimd.memset(one[:], 1.0)
        warm = const.tile([P, 1], F32, name="warm")
        nc.scalar.activation(out=warm[:], in_=one[:], func=ACT.Abs_reciprocal_sqrt)

        ident = const.tile([P, P], F32, name="ident")
        make_identity(nc, ident[:])

        def load_w(i):
            wb = wbytes.tile([P, K], U8, name="wb", tag="wb")
            nc.sync.dma_start(out=wb[:], in_=w_bytes[i * P : (i + 1) * P, :])
            return wb

        def load_x(m):
            xr = rows.tile([P, K], BF16, name="xr", tag="rows")
            nc.sync.dma_start(out=xr[:], in_=x_rows[m * P : (m + 1) * P, :])
            return xr

        wb_tiles = {}
        x_tiles = {}
        for i in (0, 1):
            wb_tiles[i] = wbytes.tile([P, K], U8, name="wb", tag="wb")
        for c0, c1 in ((0, 1024), (1024, K)):
            for i in (0, 1):
                nc.sync.dma_start(out=wb_tiles[i][:, c0:c1], in_=w_bytes[i * P : (i + 1) * P, c0:c1])
        x_tiles[0] = load_x(0)
        x_tiles[1] = load_x(1)
        wb_tiles[2] = load_w(2)
        wb_tiles[3] = load_w(3)
        x_tiles[2] = load_x(2)
        x_tiles[3] = load_x(3)
        wb_tiles[4] = load_w(4)
        wb_tiles[5] = load_w(5)
        b_bc = const.tile([P, CHANNELS], BF16, name="b_bc")
        nc.sync.dma_start(out=b_bc[:], in_=b.partition_broadcast(P))

        rot = const.tile([P, M_TILES, 2 * HEAD], F32, name="rot")
        fr_v = fr_sb[:].rearrange("p m (j i l) -> p m j i l", i=2, l=2)
        g_v = g_bc[:].rearrange("p (j l) -> p j l", l=2)
        for l in (0, 1):
            nc.gpsimd.tensor_tensor(
                out=rot[:, :, l * HEAD : (l + 1) * HEAD].rearrange("p m (j i) -> p m j i", i=2),
                in0=fr_v[:, :, :, :, l],
                in1=g_v[:, :, l].unsqueeze(1).unsqueeze(3).to_broadcast([P, M_TILES, HEAD // 2, 2]),
                op=ALU.mult,
            )

        rot_turned = const.tile([P, 4 * HEAD], F32, name="rot_turned")
        rot_ps = tabs.tile([P, 4 * HEAD], F32, name="rot_ps")

        def tables_first_turn():
            bank = banks.tile([P, 512], F32, name="bank", tag="bank")
            for m in (2, 3):
                for l in (0, 1):
                    col = (2 * (m - 2) + l) * HEAD
                    nc.tensor.transpose(out=bank[:, col : col + HEAD], in_=rot[:, m, l * HEAD : (l + 1) * HEAD], identity=ident[:])
            nc.vector.tensor_copy(out=rot_turned[:], in_=bank[:])

        def tables_second_turn():
            for c in range(4):
                cols = slice(c * HEAD, (c + 1) * HEAD)
                nc.tensor.transpose(out=rot_ps[:, cols], in_=rot_turned[:, cols], identity=ident[:])

        x_codes = const.tile([P, M_TILES * PASSES * P], U32, name="x_codes", align_bytes=64)
        x_scales = const.tile([P, M_TILES * PASSES * P], U8, name="x_scales", align_bytes=64)

        def transpose_pass(two_tiles, gp):
            bank = banks.tile([P, 512], F32, name="bank", tag="bank")
            for u in (0, 1):
                for rr in (0, 1):
                    col = (2 * u + rr) * P
                    nc.tensor.transpose(
                        out=bank[:, col : col + P],
                        in_=two_tiles[rr][:].bitcast(F32)[:, 256 * gp + u : 256 * (gp + 1) : 2],
                        identity=ident[:],
                    )
            return bank

        def quantize(src, first_col, n_cols, codes, scales, first_word):
            col = first_col
            for w in quantize_widths(n_cols):
                words = slice(first_word + (col - first_col) // 4, first_word + (col - first_col + w) // 4)
                nc.vector.quantize_mx(out=codes[:, words].bitcast(FP8X4), scales=scales[:, words], in_=src[:, col : col + w])
                col += w

        def x_stage(mp):
            two = (x_tiles[2 * mp], x_tiles[2 * mp + 1])
            gx = grouped.tile([P, 2 * K], BF16, name="gx", tag="gx", bufs=1, align_bytes=64)
            for gp in range(PASSES):
                bank = transpose_pass(two, gp)
                mover = nc.vector.tensor_copy if mp == 0 and gp < 4 else nc.scalar.copy
                mover(
                    out=gx[:, gp * 1024 : (gp + 1) * 1024].bitcast(F32).rearrange("p (n u) -> p n u", u=2),
                    in_=bank[:].rearrange("p (u n) -> p n u", u=2),
                )
            quantize(gx, 0, 2 * K, x_codes, x_scales, mp * 2 * PASSES * P)

        def new_pair():
            return [rows.tile([P, K], BF16, name="wr", tag="rows") for rr in (0, 1)]

        def cast_cols(i, two, c0, c1):
            for rr in (0, 1):
                nc.scalar.copy(out=two[rr][:, c0:c1], in_=wb_tiles[i + rr][:, c0:c1].bitcast(FP8))

        def scale_out(bank, grp, n_tiles, r, gp):
            col = (gp * n_tiles + r) * 512
            nc.vector.tensor_tensor(
                out=grp[:, col : col + 1024].rearrange("p (n u e) -> p n u e", u=2, e=2),
                in0=bank[:].bitcast(BF16).rearrange("p (u n e) -> p n u e", u=2, e=2),
                in1=k_scale[:, gp, :].rearrange("p (u e) -> p u e", e=2).unsqueeze(1).to_broadcast([P, 2 * P, 2, 2]),
                op=ALU.mult,
            )

        def scale_in_place(bank, grp, n_tiles, r, gp):
            col = (gp * n_tiles + r) * 512
            nc.scalar.copy(
                out=grp[:, col : col + 1024].bitcast(F32).rearrange("p (n u) -> p n u", u=2),
                in_=bank[:].rearrange("p (u n) -> p n u", u=2),
            )
            for a in range(col, col + 1024, 1024):
                values = grp[:, a : a + 1024].rearrange("p (n t) -> p n t", t=4)
                nc.gpsimd.tensor_tensor(
                    out=values, in0=values, in1=k_scale[:, gp, :].unsqueeze(1).to_broadcast([P, 256, 4]), op=ALU.mult
                )

        def scale_out_scalar(bank, grp, n_tiles, r, gp):
            col = (gp * n_tiles + r) * 512
            dst = grp[:, col : col + 1024].rearrange("p (n t) -> p n t", t=4)
            srcv = bank[:].bitcast(BF16).rearrange("p (u n e) -> p n u e", u=2, e=2)
            for u in (0, 1):
                for e in (0, 1):
                    t = 2 * u + e
                    nc.scalar.activation(out=dst[:, :, t], in_=srcv[:, :, u, e], func=ACT.Copy, scale=k_scale[:, gp, t : t + 1])

        waiting = []
        finished = [0]
        held = []

        def project(gi, first, n_tiles, m, acc):
            width = n_tiles * P
            c0 = first * P
            last = gi == LAST
            pr = proj.tile([P, width], F32, name="pr", tag="pr")
            nc.vector.tensor_tensor(out=pr[:], in0=acc, in1=b_bc[:, c0 : c0 + width], op=ALU.add)
            ss = small.tile([P, n_tiles], F32, name="ss", tag="ss")
            for h in range(n_tiles):
                junk = small.tile([P, HEAD], F32, name="junk", tag="junk")
                nc.scalar.activation(
                    out=junk[:], in_=pr[:, h * HEAD : (h + 1) * HEAD], func=ACT.Square, accum_out=ss[:, h : h + 1]
                )
            rinv = small.tile([P, n_tiles], F32, name="rinv", tag="rinv")
            nc.scalar.activation(out=rinv[:], in_=ss[:], func=ACT.Abs_reciprocal_sqrt, bias=EPS, scale=1.0 / HEAD)
            unit = (gi, pr, rinv, n_tiles, m, c0)
            if last:
                last_units.append(unit)
            elif m == 3 and gi < 4:
                held_all.append(unit)
            else:
                rotate(unit)

        held_all = []
        last_units = []

        def rotate(unit):
            gi, pr, rinv, n_tiles, m, c0 = unit
            last = gi == LAST
            helped = (m >= 2 and gi >= 4)
            eng = nc.vector if last and m != 1 else nc.gpsimd
            width = n_tiles * P
            shape5 = [P, 2, n_tiles, HEAD // 2, 2]
            terms = epi.tile([P, 2, width], F32, name="terms", tag="terms")
            table = rot_ps[:, 2 * (m - 2) * HEAD : 2 * (m - 1) * HEAD] if helped else rot[:, m, :]
            (nc.vector if helped else eng).tensor_tensor(
                out=terms[:].rearrange("p l (h j i) -> p l h j i", h=n_tiles, i=2),
                in0=pr[:].rearrange("p (h j l) -> p l h j", h=n_tiles, l=2).unsqueeze(4).to_broadcast(shape5),
                in1=table.rearrange("p (l j i) -> p l j i", l=2, i=2).unsqueeze(2).to_broadcast(shape5),
                op=ALU.mult,
            )
            unit = (eng, terms, rinv, n_tiles, m, c0)
            if m == 3 and gi >= 4 and not last:
                held.append(unit)
            else:
                add_terms(unit)

        def add_terms(unit):
            eng, terms, rinv, n_tiles, m, c0 = unit
            eng.tensor_tensor(out=terms[:, 0, :], in0=terms[:, 0, :], in1=terms[:, 1, :], op=ALU.add)
            close(terms[:, 0, :], terms[:, 0, :], rinv, n_tiles, m, c0)

        def close(src, res, rinv, n_tiles, m, c0):
            waiting.append((src, res, rinv, n_tiles, m, c0))
            if len(waiting) - finished[0] > 1:
                finish()

        def finish():
            src, res, rinv, n_tiles, m, c0 = waiting[finished[0]]
            finished[0] += 1
            for h in range(n_tiles):
                cols = slice(h * HEAD, (h + 1) * HEAD)
                nc.scalar.activation(out=res[:, cols], in_=src[:, cols], func=ACT.Copy, scale=rinv[:, h : h + 1])
            nc.sync.dma_start(out=out_rows[m * P : (m + 1) * P, c0 : c0 + n_tiles * P], in_=res)

        def release_held(codes):
            if held or held_all:
                seen = small.tile([P, 1], U32, name="seen", tag="seen")
                nc.gpsimd.tensor_copy(out=seen[:], in_=codes[:, codes.shape[1] - 1 :])
                for unit in held:
                    add_terms(unit)
                held.clear()
                for unit in held_all:
                    rotate(unit)
                held_all.clear()

        open_acc = {}

        def warm_up(src, count):
            acc_tile = accs.tile([P, 512], F32, name="acc", tag="acc")
            end = src.shape[1]
            for q in range(count):
                nc.tensor.matmul(out=acc_tile[:], lhsT=src[:, end - P :], rhs=src[:, end - 512 :], start=True, stop=True)

        def run_pass(item):
            gi, first, n_tiles, codes, scales, m, gp = item
            width = n_tiles * P
            if gp == 0:
                if gi == LAST and m >= 2:
                    spare = banks.tile([P, 512], F32, name="bank", tag="bank")
                    open_acc[m] = spare[:, :width]
                else:
                    acc_tile = accs.tile([P, width], F32, name="acc", tag="acc")
                    open_acc[m] = acc_tile[:, :]
            acc = open_acc[m]
            xw = ((m // 2) * 2 * PASSES + gp * 2 + m % 2) * P
            xc = slice(xw, xw + P)
            wc = slice(gp * width, (gp + 1) * width)
            nc.tensor.matmul_mx(
                out=acc,
                lhsT=x_codes[:, xc].bitcast(FP8X4),
                lhsT_scale=x_scales[:, xc],
                rhs=codes[:, wc].bitcast(FP8X4),
                rhs_scale=scales[:, wc],
                start=(gp == 0),
                stop=(gp == PASSES - 1),
            )
            if gp == PASSES - 1:
                project(gi, first, n_tiles, m, acc)

        todo = []
        st = {"done": 0, "first": 0, "grp": None}

        def run_group(gi):
            n_tiles = GROUP_TILES[gi]
            first = st["first"]
            last = gi == LAST
            before = st["grp"]
            grp = grouped.tile([P, PASSES * n_tiles * 512], BF16, name="grp", tag="grp", align_bytes=64)
            codes = wq.tile([P, PASSES * n_tiles * P], U32, name="w_codes", tag="w_codes", align_bytes=64)
            scales = wq.tile([P, PASSES * n_tiles * P], U8, name="w_scales", tag="w_scales", align_bytes=64)
            stops = (1,2,4,5,7,8,10,11) if n_tiles == 4 else (2, 4)
            slots = len(stops)
            for r in range(0, n_tiles, 2):
                i = first + r
                for j in (i + PREFETCH, i + PREFETCH + 1):
                    if j < ROW_TILES:
                        wb_tiles[j] = load_w(j)
                two = st["two_next"]
                if i + 2 < ROW_TILES:
                    st["two_next"] = new_pair()
                for gp in range(PASSES):
                    if gp % 2 == 0 and i + 2 < ROW_TILES:
                        cast_cols(i + 2, st["two_next"], gp * 512, gp * 512 + 1024)
                    bank = transpose_pass(two, gp)
                    if gi == 6 and gp == 0:
                        scale_in_place(bank, grp, n_tiles, r, gp)
                    elif gi in (1, 3) and r == 0 and gp == 0 or gi == 6 and gp == 1:
                        scale_out_scalar(bank, grp, n_tiles, r, gp)
                    else:
                        scale_out(bank, grp, n_tiles, r, gp)
                    if last and gp in (3, PASSES - 1):
                        done = 0 if gp == 3 else 4
                        quantize(grp, done * n_tiles * 512, (gp + 1 - done) * n_tiles * 512, codes, scales, done * n_tiles * P)
                    if (r // 2) * PASSES + gp in stops:
                        if gi > 0 and slots == len(stops):
                            warm_up(before, 2)
                        share = -((st["done"] - len(todo)) // slots)
                        for item in todo[st["done"] : st["done"] + share]:
                            run_pass(item)
                        st["done"] += share
                        slots -= 1
                if i < M_TILES:
                    x_stage(i // 2)
                    if i == 0:
                        tables_first_turn()
                    else:
                        tables_second_turn()
            if not last:
                quantize(grp, 0, PASSES * n_tiles * 512, codes, scales, 0)
            release_held(codes)
            for gps in (range(4), range(4, PASSES)) if last else (range(PASSES),):
                for m in range(M_TILES):
                    for gp in gps:
                        todo.append((gi, first, n_tiles, codes, scales, m, gp))
            st["first"] = first + n_tiles
            st["grp"] = grp

        with tc.manual_schedule(engines={mybir.EngineType.PE}):
            st["two_next"] = new_pair()
            for c0 in range(0, K, 512):
                first_pair = st["two_next"]
                nc.scalar.copy(out=first_pair[0][:, c0 : c0 + 512], in_=wb_tiles[0][:, c0 : c0 + 512].bitcast(FP8))
                caster = nc.vector.tensor_copy if c0 < 1 * 512 else nc.scalar.copy
                caster(out=first_pair[1][:, c0 : c0 + 512], in_=wb_tiles[1][:, c0 : c0 + 512].bitcast(FP8))
            run_group(0)
        with tc.manual_schedule(engines={mybir.EngineType.PE, mybir.EngineType.Activation, mybir.EngineType.Pool}):
            for gi in range(1, len(GROUP_TILES)):
                run_group(gi)
        with tc.manual_schedule(
            engines={mybir.EngineType.PE, mybir.EngineType.Activation, mybir.EngineType.Pool, mybir.EngineType.DVE}
        ):
            for item in todo[st["done"] :]:
                run_pass(item)
            for m in (1, 2, 3, 0):
                rotate(last_units[m])
            while finished[0] < len(waiting):
                finish()
